import numpy as np
import ml_dtypes


def mxq(x, axis, fmt="e4m3"):
    dtype, down = {"e4m3": (ml_dtypes.float8_e4m3fn, 7), "e5m2": (ml_dtypes.float8_e5m2, 14)}[fmt]
    v = np.moveaxis(np.asarray(x, np.float32).astype(ml_dtypes.bfloat16).astype(np.float64), axis, -1)
    blocks = v.reshape(v.shape[:-1] + (-1, 32))
    amax = np.abs(blocks).max(-1, keepdims=True)
    byte = np.maximum(np.where(amax > 0, np.frexp(amax)[1] - 1 + 127, 0) - down, 1)
    scale = np.exp2(byte - 127.0)
    codes = (blocks / scale).astype(np.float32).astype(dtype).astype(np.float64)
    return np.moveaxis((codes * scale).reshape(v.shape), -1, axis)


WIDE = False


def mx_kscale(k):
    if not WIDE:
        return np.ones(k)
    levels = np.array([20, -20, 10, -10, 0])
    a = np.random.permutation(np.resize(levels, k // 512 * 4)).reshape(k // 512, 4)
    idx = np.arange(k)
    return np.exp2(a[idx // 512, idx % 128 // 32])


BF16 = ml_dtypes.bfloat16


def bf(x):
    return np.asarray(x, np.float32).astype(BF16)


def f64(x):
    return np.asarray(x).astype(np.float64)


B, J, I, O = 2048, 3, 512, 512
IN_CH = J * I
OUT_CH = J * O
NEIGHBOUR_LIST = [[j for j in (i - 1, i, i + 1) if 0 <= j < J] for i in range(J)]


def build_mask():
    mask = np.zeros((OUT_CH, IN_CH))
    for i, neigh in enumerate(NEIGHBOUR_LIST):
        mask[i * O:(i + 1) * O, neigh[0] * I:(neigh[-1] + 1) * I] = 1.0
    return mask


def setup_inputs():
    u = mx_kscale(OUT_CH)
    keep = np.random.random((OUT_CH, IN_CH)) < 0.75
    x = np.random.standard_normal((B, IN_CH))
    weight = np.random.standard_normal((OUT_CH, IN_CH)) / np.sqrt(0.75 * 3 * I) / u[:, None]
    bias = np.random.standard_normal(OUT_CH) * 0.5
    g = np.random.standard_normal((B, OUT_CH)) * np.exp2(np.random.randint(-12, 1, (B, 1))) * 4.0 * u[None, :]
    return {"x": bf(x),
            "weight": bf(weight),
            "mask": bf(build_mask() * keep),
            "bias": bf(bias),
            "grad_out": bf(g)}


def reference(x, weight, mask, bias, grad_out):
    w = f64(weight) * f64(mask)
    gq = mxq(f64(grad_out), 1, "e5m2")
    cols = []
    for k in range(J):
        outs = [i for i, neigh in enumerate(NEIGHBOUR_LIST) if k in neigh]
        lo, hi = outs[0] * O, (outs[-1] + 1) * O
        cols.append(gq[:, lo:hi] @ mxq(w[lo:hi, k * I:(k + 1) * I], 0, "e4m3"))
    return np.concatenate(cols, axis=1)

@@ -1,0 +1,168 @@
+from contextlib import ExitStack
+
+import concourse.mybir as mybir
+from concourse.masks import make_identity
+
+F32 = mybir.dt.float32
+BF16 = mybir.dt.bfloat16
+U32 = mybir.dt.uint32
+U8 = mybir.dt.uint8
+E4M3X4 = mybir.dt.float8_e4m3fn_x4
+E5M2X4 = mybir.dt.float8_e5m2_x4
+
+P = 128
+PACK = 4
+JOINTS = 3
+CH = 512
+WIDTH = JOINTS * CH
+TOKENS = 2048
+TILES = TOKENS // P
+PAIRS = TILES // 2
+HALF = CH // 2
+BLOCKS = 7
+
+FLOPS = 2 * TOKENS * CH * CH * BLOCKS
+BYTES = 2 * TOKENS * WIDTH + 2 * 2 * BLOCKS * CH * CH + 4 * TOKENS * WIDTH
+
+
+def neighbours(joint):
+    return [j for j in (joint - 1, joint, joint + 1) if 0 <= j < JOINTS]
+
+
+def tile_skeletonlinear_t_kernel(tc, x, weight, mask, bias, grad_out, out):
+    nc = tc.nc
+    grad_tiles = grad_out.rearrange("(p t) c -> p t c", t=TILES)
+    out_tiles = out.rearrange("(p t) c -> p t c", t=TILES)
+
+    with ExitStack() as pools:
+        keep = pools.enter_context(tc.tile_pool(name="keep", bufs=1))
+        grad_stage = pools.enter_context(tc.tile_pool(name="grad_stage", bufs=4))
+        w_stage = pools.enter_context(tc.tile_pool(name="w_stage", bufs=2))
+        results = pools.enter_context(tc.tile_pool(name="results", bufs=8))
+        flipped = pools.enter_context(tc.psum_pool(name="flipped", bufs=4))
+        sums = pools.enter_context(tc.psum_pool(name="sums", bufs=4))
+
+        identity = keep.tile([P, P], F32)
+        make_identity(nc, identity[:])
+
+        grad_codes = keep.tile([P, JOINTS, TOKENS], U32, align_bytes=64)
+        grad_scales = keep.tile([P, JOINTS, TOKENS], U8, align_bytes=64)
+        w_codes = {}
+        w_scales = {}
+        for r in range(JOINTS):
+            for k in neighbours(r):
+                w_codes[(r, k)] = keep.tile([P, CH], U32, align_bytes=64, name="w_codes_%d_%d" % (r, k))
+                w_scales[(r, k)] = keep.tile([P, CH], U8, align_bytes=64, name="w_scales_%d_%d" % (r, k))
+
+        grad_raw = {}
+        w_raw = {}
+
+        def load_pair(i):
+            raw = keep.tile([P, 2 * WIDTH], BF16, name="grad_raw_%d" % i)
+            nc.sync.dma_start(
+                out=raw[:].rearrange("p (a c) -> p a c", a=2), in_=grad_tiles[:, 2 * i : 2 * i + 2, :]
+            )
+            grad_raw[i] = raw
+
+        def load_row_block(r):
+            cols = neighbours(r)
+            first, width = cols[0] * CH, len(cols) * CH
+            weight_rows = keep.tile([P, PACK, width], BF16, name="weight_raw_%d" % r)
+            mask_rows = keep.tile([P, PACK, width], BF16, name="mask_raw_%d" % r)
+            for u in range(2):
+                top = r * CH + u * HALF
+                for raw, source in ((weight_rows, weight), (mask_rows, mask)):
+                    nc.sync.dma_start(
+                        out=raw[:, 2 * u : 2 * u + 2, :],
+                        in_=source[top : top + HALF, first : first + width].rearrange("(p e) c -> p e c", e=2),
+                    )
+            w_raw[r] = (weight_rows, mask_rows)
+
+        def prepare_w(r, k, h):
+            weight_rows, mask_rows = w_raw[r]
+            first = (k - neighbours(r)[0]) * CH + h * HALF
+            grouped = w_stage.tile([P, HALF, PACK], BF16, align_bytes=64)
+            nc.vector.tensor_tensor(
+                out=grouped[:],
+                in0=weight_rows[:, :, first : first + HALF].rearrange("p t c -> p c t"),
+                in1=mask_rows[:, :, first : first + HALF].rearrange("p t c -> p c t"),
+                op=mybir.AluOpType.mult,
+            )
+            part = slice(h * HALF, (h + 1) * HALF)
+            nc.vector.quantize_mx(
+                out=w_codes[(r, k)][:, part].bitcast(E4M3X4),
+                scales=w_scales[(r, k)][:, part],
+                in_=grouped[:].rearrange("p c t -> p (c t)"),
+            )
+
+        def prepare_grad(i):
+            words = grad_raw[i][:].bitcast(F32)
+            for g in range(JOINTS):
+                bank = flipped.tile([P, 4 * P], F32)
+                for a in range(2):
+                    for u in range(2):
+                        first = a * (WIDTH // 2) + g * HALF + u * P
+                        nc.tensor.transpose(
+                            out=bank[:, (2 * a + u) * P : (2 * a + u + 1) * P],
+                            in_=words[:, first : first + P],
+                            identity=identity[:],
+                        )
+                grouped = grad_stage.tile([P, 2 * P * PACK], BF16, align_bytes=64)
+                nc.scalar.copy(
+                    out=grouped[:].bitcast(F32).rearrange("p (a r u) -> p a r u", a=2, u=2),
+                    in_=bank[:].rearrange("p (a u r) -> p a r u", a=2, u=2),
+                )
+                columns = slice(2 * i * P, (2 * i + 2) * P)
+                nc.vector.quantize_mx(
+                    out=grad_codes[:, g, columns].bitcast(E5M2X4),
+                    scales=grad_scales[:, g, columns],
+                    in_=grouped[:],
+                )
+
+        def multiply_pair(i, k):
+            result = results.tile([P, 2, CH], F32)
+            rows = neighbours(k)
+            for a in range(2):
+                columns = slice((2 * i + a) * P, (2 * i + a + 1) * P)
+                acc = sums.tile([P, CH], F32)
+                for r in rows:
+                    nc.tensor.matmul_mx(
+                        out=acc[:],
+                        lhsT=grad_codes[:, r, columns].bitcast(E5M2X4),
+                        lhsT_scale=grad_scales[:, r, columns],
+                        rhs=w_codes[(r, k)][:].bitcast(E4M3X4),
+                        rhs_scale=w_scales[(r, k)][:],
+                        start=(r == rows[0]),
+                        stop=(r == rows[-1]),
+                    )
+                if a == 0:
+                    nc.scalar.copy(out=result[:, a, :], in_=acc[:])
+                else:
+                    nc.vector.tensor_copy(out=result[:, a, :], in_=acc[:])
+            nc.sync.dma_start(out=out_tiles[:, 2 * i : 2 * i + 2, k * CH : (k + 1) * CH], in_=result[:])
+
+        load_pair(0)
+        load_row_block(0)
+        load_row_block(1)
+        for i in range(1, PAIRS):
+            load_pair(i)
+        load_row_block(2)
+
+        prepare_grad(0)
+        head = [(0, 0), (0, 1), (1, 0)]
+        for r, k in head:
+            for h in range(2):
+                prepare_w(r, k, h)
+        prepare_grad(1)
+
+        for k in range(JOINTS):
+            coming = [(r, k + 1, h) for r in neighbours(k + 1) if (r, k + 1) not in head for h in range(2)]
+            if k + 1 == JOINTS:
+                coming = []
+            quiet = PAIRS - len(coming)
+            for i in range(PAIRS):
+                multiply_pair(i, k)
+                if k == 0 and i + 2 < PAIRS:
+                    prepare_grad(i + 2)
+                if i >= quiet:
+                    prepare_w(*coming[i - quiet])

@@ -36,11 +36,11 @@ def tile_skeletonlinear_t_kernel(tc, x, weight, mask, bias, grad_out, out):
 
     with ExitStack() as pools:
         keep = pools.enter_context(tc.tile_pool(name="keep", bufs=1))
-        grad_stage = pools.enter_context(tc.tile_pool(name="grad_stage", bufs=4))
+        grad_stage = pools.enter_context(tc.tile_pool(name="grad_stage", bufs=6))
         w_stage = pools.enter_context(tc.tile_pool(name="w_stage", bufs=2))
         results = pools.enter_context(tc.tile_pool(name="results", bufs=8))
-        flipped = pools.enter_context(tc.psum_pool(name="flipped", bufs=4))
-        sums = pools.enter_context(tc.psum_pool(name="sums", bufs=4))
+        flipped = pools.enter_context(tc.psum_pool(name="flipped", bufs=3))
+        sums = pools.enter_context(tc.psum_pool(name="sums", bufs=5))
 
         identity = keep.tile([P, P], F32)
         make_identity(nc, identity[:])
@@ -54,21 +54,22 @@ def tile_skeletonlinear_t_kernel(tc, x, weight, mask, bias, grad_out, out):
                 w_codes[(r, k)] = keep.tile([P, CH], U32, align_bytes=64, name="w_codes_%d_%d" % (r, k))
                 w_scales[(r, k)] = keep.tile([P, CH], U8, align_bytes=64, name="w_scales_%d_%d" % (r, k))
 
-        grad_raw = {}
+        grad_words = {}
         w_raw = {}
 
-        def load_pair(i):
-            raw = keep.tile([P, 2 * WIDTH], BF16, name="grad_raw_%d" % i)
+        def load_grad(first, count):
+            raw = keep.tile([P, count * WIDTH], BF16, name="grad_raw_%d" % first)
             nc.sync.dma_start(
-                out=raw[:].rearrange("p (a c) -> p a c", a=2), in_=grad_tiles[:, 2 * i : 2 * i + 2, :]
+                out=raw[:].rearrange("p (a c) -> p a c", a=count), in_=grad_tiles[:, first : first + count, :]
             )
-            grad_raw[i] = raw
+            words = raw[:].bitcast(F32)
+            for a in range(count):
+                grad_words[first + a] = words[:, a * (WIDTH // 2) : (a + 1) * (WIDTH // 2)]
 
-        def load_row_block(r):
-            cols = neighbours(r)
+        def load_w(r, cols):
             first, width = cols[0] * CH, len(cols) * CH
-            weight_rows = keep.tile([P, PACK, width], BF16, name="weight_raw_%d" % r)
-            mask_rows = keep.tile([P, PACK, width], BF16, name="mask_raw_%d" % r)
+            weight_rows = keep.tile([P, PACK, width], BF16, name="weight_raw_%d_%d" % (r, cols[0]))
+            mask_rows = keep.tile([P, PACK, width], BF16, name="mask_raw_%d_%d" % (r, cols[0]))
             for u in range(2):
                 top = r * CH + u * HALF
                 for raw, source in ((weight_rows, weight), (mask_rows, mask)):
@@ -76,11 +77,12 @@ def tile_skeletonlinear_t_kernel(tc, x, weight, mask, bias, grad_out, out):
                         out=raw[:, 2 * u : 2 * u + 2, :],
                         in_=source[top : top + HALF, first : first + width].rearrange("(p e) c -> p e c", e=2),
                     )
-            w_raw[r] = (weight_rows, mask_rows)
+            for n, k in enumerate(cols):
+                w_raw[(r, k)] = (weight_rows, mask_rows, n * CH)
 
         def prepare_w(r, k, h):
-            weight_rows, mask_rows = w_raw[r]
-            first = (k - neighbours(r)[0]) * CH + h * HALF
+            weight_rows, mask_rows, base = w_raw[(r, k)]
+            first = base + h * HALF
             grouped = w_stage.tile([P, HALF, PACK], BF16, align_bytes=64)
             nc.vector.tensor_tensor(
                 out=grouped[:],
@@ -95,16 +97,18 @@ def tile_skeletonlinear_t_kernel(tc, x, weight, mask, bias, grad_out, out):
                 in_=grouped[:].rearrange("p c t -> p (c t)"),
             )
 
+        def prepare_block(r, k):
+            for h in range(2):
+                prepare_w(r, k, h)
+
         def prepare_grad(i):
-            words = grad_raw[i][:].bitcast(F32)
             for g in range(JOINTS):
                 bank = flipped.tile([P, 4 * P], F32)
                 for a in range(2):
                     for u in range(2):
-                        first = a * (WIDTH // 2) + g * HALF + u * P
                         nc.tensor.transpose(
                             out=bank[:, (2 * a + u) * P : (2 * a + u + 1) * P],
-                            in_=words[:, first : first + P],
+                            in_=grad_words[2 * i + a][:, g * HALF + u * P : g * HALF + (u + 1) * P],
                             identity=identity[:],
                         )
                 grouped = grad_stage.tile([P, 2 * P * PACK], BF16, align_bytes=64)
@@ -119,50 +123,84 @@ def tile_skeletonlinear_t_kernel(tc, x, weight, mask, bias, grad_out, out):
                     in_=grouped[:],
                 )
 
-        def multiply_pair(i, k):
-            result = results.tile([P, 2, CH], F32)
+        def multiply_tile(t, k, result, engine):
             rows = neighbours(k)
-            for a in range(2):
-                columns = slice((2 * i + a) * P, (2 * i + a + 1) * P)
-                acc = sums.tile([P, CH], F32)
-                for r in rows:
-                    nc.tensor.matmul_mx(
-                        out=acc[:],
-                        lhsT=grad_codes[:, r, columns].bitcast(E5M2X4),
-                        lhsT_scale=grad_scales[:, r, columns],
-                        rhs=w_codes[(r, k)][:].bitcast(E4M3X4),
-                        rhs_scale=w_scales[(r, k)][:],
-                        start=(r == rows[0]),
-                        stop=(r == rows[-1]),
-                    )
-                if a == 0:
-                    nc.scalar.copy(out=result[:, a, :], in_=acc[:])
-                else:
-                    nc.vector.tensor_copy(out=result[:, a, :], in_=acc[:])
-            nc.sync.dma_start(out=out_tiles[:, 2 * i : 2 * i + 2, k * CH : (k + 1) * CH], in_=result[:])
+            columns = slice(t * P, (t + 1) * P)
+            acc = sums.tile([P, CH], F32)
+            for r in rows:
+                nc.tensor.matmul_mx(
+                    out=acc[:],
+                    lhsT=grad_codes[:, r, columns].bitcast(E5M2X4),
+                    lhsT_scale=grad_scales[:, r, columns],
+                    rhs=w_codes[(r, k)][:].bitcast(E4M3X4),
+                    rhs_scale=w_scales[(r, k)][:],
+                    start=(r == rows[0]),
+                    stop=(r == rows[-1]),
+                )
+            if engine == "scalar":
+                nc.scalar.copy(out=result, in_=acc[:])
+            else:
+                nc.vector.tensor_copy(out=result, in_=acc[:])
 
-        load_pair(0)
-        load_row_block(0)
-        load_row_block(1)
-        for i in range(1, PAIRS):
-            load_pair(i)
-        load_row_block(2)
+        def multiply_pair(i, k, result, at, engines):
+            for a in range(2):
+                multiply_tile(2 * i + a, k, result[:, a, at : at + CH], engines[a])
+
+        def store_pair(i, first, width, result):
+            nc.sync.dma_start(out=out_tiles[:, 2 * i : 2 * i + 2, first : first + width], in_=result[:])
+
+        def prepare_w_scalar(r, k, h):
+            weight_rows, mask_rows, base = w_raw[(r, k)]
+            first = base + h * HALF
+            masked = w_stage.tile([P, PACK, HALF], BF16)
+            nc.vector.tensor_tensor(
+                out=masked[:],
+                in0=weight_rows[:, :, first : first + HALF],
+                in1=mask_rows[:, :, first : first + HALF],
+                op=mybir.AluOpType.mult,
+            )
+            regrouped = w_stage.tile([P, HALF, PACK], BF16, align_bytes=64)
+            nc.scalar.copy(out=regrouped[:], in_=masked[:].rearrange("p t c -> p c t"))
+            part = slice(h * HALF, (h + 1) * HALF)
+            nc.vector.quantize_mx(
+                out=w_codes[(r, k)][:, part].bitcast(E4M3X4),
+                scales=w_scales[(r, k)][:, part],
+                in_=regrouped[:].rearrange("p c t -> p (c t)"),
+            )
+
+        load_w(0, [0, 1])
+        load_grad(0, 2)
+        load_w(1, [0])
+        load_grad(2, 2)
+        load_grad(4, 4)
+        load_grad(8, 4)
+        load_w(1, [1, 2])
+        load_grad(12, 4)
+        load_w(2, [1, 2])
+
+        by_scalar = ((0, 1, 0), (2, 1, 0))
+
+        def prepare_half(r, k, h):
+            if (r, k, h) in by_scalar:
+                prepare_w_scalar(r, k, h)
+            else:
+                prepare_w(r, k, h)
 
         prepare_grad(0)
-        head = [(0, 0), (0, 1), (1, 0)]
-        for r, k in head:
+        for r, k in ((0, 0), (1, 0)):
             for h in range(2):
-                prepare_w(r, k, h)
-        prepare_grad(1)
+                prepare_half(r, k, h)
+        for i in range(1, 3):
+            prepare_grad(i)
 
+        coming = [(r, k, h) for r, k in ((1, 1), (0, 1), (2, 1), (1, 2), (2, 2)) for h in range(2)]
         for k in range(JOINTS):
-            coming = [(r, k + 1, h) for r in neighbours(k + 1) if (r, k + 1) not in head for h in range(2)]
-            if k + 1 == JOINTS:
-                coming = []
-            quiet = PAIRS - len(coming)
             for i in range(PAIRS):
-                multiply_pair(i, k)
-                if k == 0 and i + 2 < PAIRS:
-                    prepare_grad(i + 2)
-                if i >= quiet:
-                    prepare_w(*coming[i - quiet])
+                if k == 0 and i + 3 < PAIRS:
+                    prepare_grad(i + 3)
+                result = results.tile([P, 2, CH], F32)
+                multiply_pair(i, k, result, 0, (("vector", "scalar"), ("scalar", "scalar"), ("vector", "scalar"))[k])
+                store_pair(i, k * CH, CH, result)
+                step = k * PAIRS + i - 0
+                if 0 <= step < len(coming):
+                    prepare_half(*coming[step])

@@ -37,8 +37,10 @@ def tile_skeletonlinear_t_kernel(tc, x, weight, mask, bias, grad_out, out):
     with ExitStack() as pools:
         keep = pools.enter_context(tc.tile_pool(name="keep", bufs=1))
         grad_stage = pools.enter_context(tc.tile_pool(name="grad_stage", bufs=6))
-        w_stage = pools.enter_context(tc.tile_pool(name="w_stage", bufs=2))
-        results = pools.enter_context(tc.tile_pool(name="results", bufs=8))
+        w_stage = pools.enter_context(tc.tile_pool(name="w_stage", bufs=4))
+        results = pools.enter_context(tc.tile_pool(name="results", bufs=5))
+        wide_results = pools.enter_context(tc.tile_pool(name="wide_results", bufs=4))
+        mask_stage = pools.enter_context(tc.tile_pool(name="mask_stage", bufs=2))
         flipped = pools.enter_context(tc.psum_pool(name="flipped", bufs=3))
         sums = pools.enter_context(tc.psum_pool(name="sums", bufs=5))
 
@@ -80,28 +82,43 @@ def tile_skeletonlinear_t_kernel(tc, x, weight, mask, bias, grad_out, out):
             for n, k in enumerate(cols):
                 w_raw[(r, k)] = (weight_rows, mask_rows, n * CH)
 
-        def prepare_w(r, k, h):
+        grouped_w = {}
+        banks = {}
+        grouped_grad = {}
+        accs = {}
+        tiles = {}
+
+        def mask_w(r, k, h):
             weight_rows, mask_rows, base = w_raw[(r, k)]
             first = base + h * HALF
             grouped = w_stage.tile([P, HALF, PACK], BF16, align_bytes=64)
-            nc.vector.tensor_tensor(
-                out=grouped[:],
-                in0=weight_rows[:, :, first : first + HALF].rearrange("p t c -> p c t"),
-                in1=mask_rows[:, :, first : first + HALF].rearrange("p t c -> p c t"),
-                op=mybir.AluOpType.mult,
-            )
+            if (r, k, h) in ((1, 0, 0), (2, 1, 0)):
+                masked = mask_stage.tile([P, PACK, HALF], BF16)
+                nc.vector.tensor_tensor(
+                    out=masked[:],
+                    in0=weight_rows[:, :, first : first + HALF],
+                    in1=mask_rows[:, :, first : first + HALF],
+                    op=mybir.AluOpType.mult,
+                )
+                nc.scalar.copy(out=grouped[:], in_=masked[:].rearrange("p t c -> p c t"))
+            else:
+                nc.vector.tensor_tensor(
+                    out=grouped[:],
+                    in0=weight_rows[:, :, first : first + HALF].rearrange("p t c -> p c t"),
+                    in1=mask_rows[:, :, first : first + HALF].rearrange("p t c -> p c t"),
+                    op=mybir.AluOpType.mult,
+                )
+            grouped_w[(r, k, h)] = grouped
+
+        def quantise_w(r, k, h):
             part = slice(h * HALF, (h + 1) * HALF)
             nc.vector.quantize_mx(
                 out=w_codes[(r, k)][:, part].bitcast(E4M3X4),
                 scales=w_scales[(r, k)][:, part],
-                in_=grouped[:].rearrange("p c t -> p (c t)"),
+                in_=grouped_w[(r, k, h)][:].rearrange("p c t -> p (c t)"),
             )
 
-        def prepare_block(r, k):
-            for h in range(2):
-                prepare_w(r, k, h)
-
-        def prepare_grad(i):
+        def transpose_grad(i):
             for g in range(JOINTS):
                 bank = flipped.tile([P, 4 * P], F32)
                 for a in range(2):
@@ -111,96 +128,173 @@ def tile_skeletonlinear_t_kernel(tc, x, weight, mask, bias, grad_out, out):
                             in_=grad_words[2 * i + a][:, g * HALF + u * P : g * HALF + (u + 1) * P],
                             identity=identity[:],
                         )
-                grouped = grad_stage.tile([P, 2 * P * PACK], BF16, align_bytes=64)
+                banks[(i, g)] = bank
+
+        def group_grad(i):
+            for g in range(JOINTS):
+                grouped = grad_stage.tile([P, 2 * P * PACK], BF16, align_bytes=64, name="grad_grouped")
                 nc.scalar.copy(
                     out=grouped[:].bitcast(F32).rearrange("p (a r u) -> p a r u", a=2, u=2),
-                    in_=bank[:].rearrange("p (a u r) -> p a r u", a=2, u=2),
+                    in_=banks[(i, g)][:].rearrange("p (a u r) -> p a r u", a=2, u=2),
                 )
-                columns = slice(2 * i * P, (2 * i + 2) * P)
+                grouped_grad[(i, g)] = grouped
+
+        def quantise_grad(i):
+            columns = slice(2 * i * P, (2 * i + 2) * P)
+            for g in range(JOINTS):
                 nc.vector.quantize_mx(
                     out=grad_codes[:, g, columns].bitcast(E5M2X4),
                     scales=grad_scales[:, g, columns],
-                    in_=grouped[:],
+                    in_=grouped_grad[(i, g)][:],
                 )
 
-        def multiply_tile(t, k, result, engine):
-            rows = neighbours(k)
-            columns = slice(t * P, (t + 1) * P)
-            acc = sums.tile([P, CH], F32)
-            for r in rows:
-                nc.tensor.matmul_mx(
-                    out=acc[:],
-                    lhsT=grad_codes[:, r, columns].bitcast(E5M2X4),
-                    lhsT_scale=grad_scales[:, r, columns],
-                    rhs=w_codes[(r, k)][:].bitcast(E4M3X4),
-                    rhs_scale=w_scales[(r, k)][:],
-                    start=(r == rows[0]),
-                    stop=(r == rows[-1]),
-                )
-            if engine == "scalar":
-                nc.scalar.copy(out=result, in_=acc[:])
-            else:
-                nc.vector.tensor_copy(out=result, in_=acc[:])
-
-        def multiply_pair(i, k, result, at, engines):
+        def multiply(i, k, rows):
             for a in range(2):
-                multiply_tile(2 * i + a, k, result[:, a, at : at + CH], engines[a])
+                if rows[0] == neighbours(k)[0]:
+                    acc = sums.tile([P, CH], F32)
+                    accs[(i, k, a)] = acc
+                columns = slice((2 * i + a) * P, (2 * i + a + 1) * P)
+                for r in rows:
+                    nc.tensor.matmul_mx(
+                        out=accs[(i, k, a)][:],
+                        lhsT=grad_codes[:, r, columns].bitcast(E5M2X4),
+                        lhsT_scale=grad_scales[:, r, columns],
+                        rhs=w_codes[(r, k)][:].bitcast(E4M3X4),
+                        rhs_scale=w_scales[(r, k)][:],
+                        start=(r == neighbours(k)[0]),
+                        stop=(r == neighbours(k)[-1]),
+                    )
 
-        def store_pair(i, first, width, result):
-            nc.sync.dma_start(out=out_tiles[:, 2 * i : 2 * i + 2, first : first + width], in_=result[:])
+        def empty(i, k, engines):
+            first, width = stores_of(i)[k]
+            if (i, first) not in tiles:
+                pool = results if width == 1 else wide_results
+                tiles[(i, first)] = pool.tile([P, 2, width * CH], F32, name="result_%d" % width)
+            result = tiles[(i, first)]
+            at = (k - first) * CH
+            for a in range(2):
+                if engines[a] == "S":
+                    nc.scalar.copy(out=result[:, a, at : at + CH], in_=accs[(i, k, a)][:])
+                else:
+                    nc.vector.tensor_copy(out=result[:, a, at : at + CH], in_=accs[(i, k, a)][:])
 
-        def prepare_w_scalar(r, k, h):
-            weight_rows, mask_rows, base = w_raw[(r, k)]
-            first = base + h * HALF
-            masked = w_stage.tile([P, PACK, HALF], BF16)
-            nc.vector.tensor_tensor(
-                out=masked[:],
-                in0=weight_rows[:, :, first : first + HALF],
-                in1=mask_rows[:, :, first : first + HALF],
-                op=mybir.AluOpType.mult,
-            )
-            regrouped = w_stage.tile([P, HALF, PACK], BF16, align_bytes=64)
-            nc.scalar.copy(out=regrouped[:], in_=masked[:].rearrange("p t c -> p c t"))
-            part = slice(h * HALF, (h + 1) * HALF)
-            nc.vector.quantize_mx(
-                out=w_codes[(r, k)][:, part].bitcast(E4M3X4),
-                scales=w_scales[(r, k)][:, part],
-                in_=regrouped[:].rearrange("p c t -> p (c t)"),
-            )
-
-        load_w(0, [0, 1])
-        load_grad(0, 2)
-        load_w(1, [0])
-        load_grad(2, 2)
-        load_grad(4, 4)
-        load_grad(8, 4)
-        load_w(1, [1, 2])
-        load_grad(12, 4)
-        load_w(2, [1, 2])
-
-        by_scalar = ((0, 1, 0), (2, 1, 0))
-
-        def prepare_half(r, k, h):
-            if (r, k, h) in by_scalar:
-                prepare_w_scalar(r, k, h)
+        def store(i, first):
+            width = stores_of(i)[first][1]
+            columns = slice(first * CH, (first + width) * CH)
+            if i < PAIRS - 1:
+                nc.sync.dma_start(out=out_tiles[:, 2 * i : 2 * i + 2, columns], in_=tiles[(i, first)][:])
             else:
-                prepare_w(r, k, h)
+                for a in range(2):
+                    nc.sync.dma_start(out=out_tiles[:, 2 * i + a, columns], in_=tiles[(i, first)][:, a, :])
 
-        prepare_grad(0)
-        for r, k in ((0, 0), (1, 0)):
-            for h in range(2):
-                prepare_half(r, k, h)
-        for i in range(1, 3):
-            prepare_grad(i)
+        def stores_of(i):
+            if i < 2:
+                return ((0, 2), (0, 2), (2, 1))
+            return ((0, 1), (1, 2), (1, 2))
 
-        coming = [(r, k, h) for r, k in ((1, 1), (0, 1), (2, 1), (1, 2), (2, 2)) for h in range(2)]
-        for k in range(JOINTS):
-            for i in range(PAIRS):
-                if k == 0 and i + 3 < PAIRS:
-                    prepare_grad(i + 3)
-                result = results.tile([P, 2, CH], F32)
-                multiply_pair(i, k, result, 0, (("vector", "scalar"), ("scalar", "scalar"), ("vector", "scalar"))[k])
-                store_pair(i, k * CH, CH, result)
-                step = k * PAIRS + i - 0
-                if 0 <= step < len(coming):
-                    prepare_half(*coming[step])
+        with tc.manual_schedule():
+            load_w(0, [0, 1])
+            load_grad(0, 2)
+            load_w(1, [0, 1, 2])
+            load_grad(2, 2)
+            load_grad(4, 4)
+            load_w(2, [1, 2])
+            load_grad(8, 4)
+            load_grad(12, 4)
+
+            transpose_grad(0)
+            group_grad(0)
+            mask_w(0, 0, 0)
+            mask_w(0, 0, 1)
+            quantise_w(0, 0, 0)
+            quantise_w(0, 0, 1)
+            quantise_grad(0)
+            mask_w(0, 1, 0)
+            mask_w(0, 1, 1)
+            quantise_w(0, 1, 0)
+            quantise_w(0, 1, 1)
+
+            mask_w(1, 0, 0)
+            mask_w(1, 0, 1)
+            transpose_grad(1)
+            group_grad(1)
+            quantise_w(1, 0, 1)
+            quantise_w(1, 0, 0)
+            mask_w(1, 1, 0)
+            quantise_grad(1)
+
+            multiply(0, 0, (0, 1))
+            multiply(1, 0, (0, 1))
+            transpose_grad(2)
+            transpose_grad(3)
+            empty(0, 0, "VS")
+            quantise_w(1, 1, 0)
+            mask_w(1, 1, 1)
+            empty(1, 0, "VS")
+            group_grad(2)
+            quantise_grad(2)
+            group_grad(3)
+            quantise_w(1, 1, 1)
+            quantise_grad(3)
+            multiply(2, 0, (0, 1))
+            multiply(3, 0, (0, 1))
+            empty(2, 0, "SS")
+
+            mask_w(2, 1, 0)
+            empty(3, 0, "SS")
+            mask_w(2, 1, 1)
+            multiply(0, 1, (0, 1))
+            multiply(1, 1, (0, 1))
+            quantise_w(2, 1, 0)
+            quantise_w(2, 1, 1)
+            mask_w(1, 2, 0)
+            mask_w(1, 2, 1)
+            multiply(0, 1, (2,))
+            multiply(1, 1, (2,))
+            quantise_w(1, 2, 0)
+            quantise_w(1, 2, 1)
+            empty(0, 1, "SS")
+            empty(1, 1, "SS")
+            mask_w(2, 2, 0)
+            mask_w(2, 2, 1)
+            store(2, 0)
+            store(3, 0)
+            store(0, 0)
+            store(1, 0)
+            multiply(2, 1, (0, 1, 2))
+            multiply(3, 1, (0, 1, 2))
+            transpose_grad(4)
+            quantise_w(2, 2, 0)
+            quantise_w(2, 2, 1)
+            empty(2, 1, "SS")
+            group_grad(4)
+            quantise_grad(4)
+            empty(3, 1, "SS")
+            multiply(0, 2, (1, 2))
+            multiply(1, 2, (1, 2))
+            transpose_grad(5)
+            empty(0, 2, "VS")
+            store(0, 2)
+            empty(1, 2, "VS")
+            store(1, 2)
+            multiply(2, 2, (1, 2))
+            multiply(3, 2, (1, 2))
+            group_grad(5)
+            empty(2, 2, "VS")
+            store(2, 1)
+            quantise_grad(5)
+            empty(3, 2, "VS")
+            store(3, 1)
+
+            for i in range(4, PAIRS):
+                for k in range(JOINTS):
+                    multiply(i, k, neighbours(k))
+                    if k == 1 and i + 2 < PAIRS:
+                        transpose_grad(i + 2)
+                    empty(i, k, ("VS", "SS", "VS")[k])
+                    if k == 1 and i + 2 < PAIRS:
+                        group_grad(i + 2)
+                    if k == 2 and i + 2 < PAIRS:
+                        quantise_grad(i + 2)
+                    if k + 1 == sum(stores_of(i)[k]):
+                        store(i, stores_of(i)[k][0])

@@ -36,9 +36,9 @@ def tile_skeletonlinear_t_kernel(tc, x, weight, mask, bias, grad_out, out):
 
     with ExitStack() as pools:
         keep = pools.enter_context(tc.tile_pool(name="keep", bufs=1))
-        grad_stage = pools.enter_context(tc.tile_pool(name="grad_stage", bufs=6))
+        grad_stage = pools.enter_context(tc.tile_pool(name="grad_stage", bufs=3))
         w_stage = pools.enter_context(tc.tile_pool(name="w_stage", bufs=4))
-        results = pools.enter_context(tc.tile_pool(name="results", bufs=5))
+        results = pools.enter_context(tc.tile_pool(name="results", bufs=4))
         wide_results = pools.enter_context(tc.tile_pool(name="wide_results", bufs=4))
         mask_stage = pools.enter_context(tc.tile_pool(name="mask_stage", bufs=2))
         flipped = pools.enter_context(tc.psum_pool(name="flipped", bufs=3))
@@ -47,8 +47,8 @@ def tile_skeletonlinear_t_kernel(tc, x, weight, mask, bias, grad_out, out):
         identity = keep.tile([P, P], F32)
         make_identity(nc, identity[:])
 
-        grad_codes = keep.tile([P, JOINTS, TOKENS], U32, align_bytes=64)
-        grad_scales = keep.tile([P, JOINTS, TOKENS], U8, align_bytes=64)
+        grad_codes = keep.tile([P, PAIRS, JOINTS * 2 * P], U32, align_bytes=64)
+        grad_scales = keep.tile([P, PAIRS, JOINTS * 2 * P], U8, align_bytes=64)
         w_codes = {}
         w_scales = {}
         for r in range(JOINTS):
@@ -88,34 +88,33 @@ def tile_skeletonlinear_t_kernel(tc, x, weight, mask, bias, grad_out, out):
         accs = {}
         tiles = {}
 
-        def mask_w(r, k, h):
+        def mask_w(r, k):
             weight_rows, mask_rows, base = w_raw[(r, k)]
-            first = base + h * HALF
-            grouped = w_stage.tile([P, HALF, PACK], BF16, align_bytes=64)
-            if (r, k, h) in ((1, 0, 0), (2, 1, 0)):
+            grouped = w_stage.tile([P, CH, PACK], BF16, align_bytes=64)
+            grouped_w[(r, k)] = grouped
+            start = 0
+            if (r, k) in ((1, 0),):
+                start = HALF
                 masked = mask_stage.tile([P, PACK, HALF], BF16)
                 nc.vector.tensor_tensor(
                     out=masked[:],
-                    in0=weight_rows[:, :, first : first + HALF],
-                    in1=mask_rows[:, :, first : first + HALF],
+                    in0=weight_rows[:, :, base : base + HALF],
+                    in1=mask_rows[:, :, base : base + HALF],
                     op=mybir.AluOpType.mult,
                 )
-                nc.scalar.copy(out=grouped[:], in_=masked[:].rearrange("p t c -> p c t"))
-            else:
-                nc.vector.tensor_tensor(
-                    out=grouped[:],
-                    in0=weight_rows[:, :, first : first + HALF].rearrange("p t c -> p c t"),
-                    in1=mask_rows[:, :, first : first + HALF].rearrange("p t c -> p c t"),
-                    op=mybir.AluOpType.mult,
-                )
-            grouped_w[(r, k, h)] = grouped
+                nc.scalar.copy(out=grouped[:, 0:HALF, :], in_=masked[:].rearrange("p t c -> p c t"))
+            nc.vector.tensor_tensor(
+                out=grouped[:, start:CH, :],
+                in0=weight_rows[:, :, base + start : base + CH].rearrange("p t c -> p c t"),
+                in1=mask_rows[:, :, base + start : base + CH].rearrange("p t c -> p c t"),
+                op=mybir.AluOpType.mult,
+            )
 
-        def quantise_w(r, k, h):
-            part = slice(h * HALF, (h + 1) * HALF)
+        def quantise_w(r, k):
             nc.vector.quantize_mx(
-                out=w_codes[(r, k)][:, part].bitcast(E4M3X4),
-                scales=w_scales[(r, k)][:, part],
-                in_=grouped_w[(r, k, h)][:].rearrange("p c t -> p (c t)"),
+                out=w_codes[(r, k)][:].bitcast(E4M3X4),
+                scales=w_scales[(r, k)][:],
+                in_=grouped_w[(r, k)][:].rearrange("p c t -> p (c t)"),
             )
 
         def transpose_grad(i):
@@ -131,21 +130,22 @@ def tile_skeletonlinear_t_kernel(tc, x, weight, mask, bias, grad_out, out):
                 banks[(i, g)] = bank
 
         def group_grad(i):
+            grouped = grad_stage.tile([P, JOINTS * 2 * P * PACK], BF16, align_bytes=64, name="grad_grouped")
+            grouped_grad[i] = grouped
+            words = grouped[:].bitcast(F32)
             for g in range(JOINTS):
-                grouped = grad_stage.tile([P, 2 * P * PACK], BF16, align_bytes=64, name="grad_grouped")
                 nc.scalar.copy(
-                    out=grouped[:].bitcast(F32).rearrange("p (a r u) -> p a r u", a=2, u=2),
+                    out=words[:, g * 4 * P : (g + 1) * 4 * P].rearrange("p (a r u) -> p a r u", a=2, u=2),
                     in_=banks[(i, g)][:].rearrange("p (a u r) -> p a r u", a=2, u=2),
                 )
-                grouped_grad[(i, g)] = grouped
 
         def quantise_grad(i):
-            columns = slice(2 * i * P, (2 * i + 2) * P)
-            for g in range(JOINTS):
+            for first, count in ((0, 2), (2, 1)):
+                columns = slice(first * 2 * P, (first + count) * 2 * P)
                 nc.vector.quantize_mx(
-                    out=grad_codes[:, g, columns].bitcast(E5M2X4),
-                    scales=grad_scales[:, g, columns],
-                    in_=grouped_grad[(i, g)][:],
+                    out=grad_codes[:, i, columns].bitcast(E5M2X4),
+                    scales=grad_scales[:, i, columns],
+                    in_=grouped_grad[i][:, first * 2 * P * PACK : (first + count) * 2 * P * PACK],
                 )
 
         def multiply(i, k, rows):
@@ -153,26 +153,26 @@ def tile_skeletonlinear_t_kernel(tc, x, weight, mask, bias, grad_out, out):
                 if rows[0] == neighbours(k)[0]:
                     acc = sums.tile([P, CH], F32)
                     accs[(i, k, a)] = acc
-                columns = slice((2 * i + a) * P, (2 * i + a + 1) * P)
                 for r in rows:
+                    columns = slice((2 * r + a) * P, (2 * r + a + 1) * P)
                     nc.tensor.matmul_mx(
                         out=accs[(i, k, a)][:],
-                        lhsT=grad_codes[:, r, columns].bitcast(E5M2X4),
-                        lhsT_scale=grad_scales[:, r, columns],
+                        lhsT=grad_codes[:, i, columns].bitcast(E5M2X4),
+                        lhsT_scale=grad_scales[:, i, columns],
                         rhs=w_codes[(r, k)][:].bitcast(E4M3X4),
                         rhs_scale=w_scales[(r, k)][:],
                         start=(r == neighbours(k)[0]),
                         stop=(r == neighbours(k)[-1]),
                     )
 
-        def empty(i, k, engines):
+        def empty(i, k, engines, parts=(0, 1)):
             first, width = stores_of(i)[k]
             if (i, first) not in tiles:
                 pool = results if width == 1 else wide_results
                 tiles[(i, first)] = pool.tile([P, 2, width * CH], F32, name="result_%d" % width)
             result = tiles[(i, first)]
             at = (k - first) * CH
-            for a in range(2):
+            for a in parts:
                 if engines[a] == "S":
                     nc.scalar.copy(out=result[:, a, at : at + CH], in_=accs[(i, k, a)][:])
                 else:
@@ -188,9 +188,16 @@ def tile_skeletonlinear_t_kernel(tc, x, weight, mask, bias, grad_out, out):
                     nc.sync.dma_start(out=out_tiles[:, 2 * i + a, columns], in_=tiles[(i, first)][:, a, :])
 
         def stores_of(i):
-            if i < 2:
-                return ((0, 2), (0, 2), (2, 1))
-            return ((0, 1), (1, 2), (1, 2))
+            if i in (2, 3):
+                return ((0, 1), (1, 2), (1, 2))
+            if i == 6:
+                return ((0, 1), (1, 1), (2, 1))
+            return ((0, 2), (0, 2), (2, 1))
+
+        def store_if_last(i, k):
+            first, width = stores_of(i)[k]
+            if k == first + width - 1:
+                store(i, first)
 
         with tc.manual_schedule():
             load_w(0, [0, 1])
@@ -204,59 +211,48 @@ def tile_skeletonlinear_t_kernel(tc, x, weight, mask, bias, grad_out, out):
 
             transpose_grad(0)
             group_grad(0)
-            mask_w(0, 0, 0)
-            mask_w(0, 0, 1)
-            quantise_w(0, 0, 0)
-            quantise_w(0, 0, 1)
+            mask_w(0, 0)
+            quantise_w(0, 0)
             quantise_grad(0)
-            mask_w(0, 1, 0)
-            mask_w(0, 1, 1)
-            quantise_w(0, 1, 0)
-            quantise_w(0, 1, 1)
+            mask_w(0, 1)
+            quantise_w(0, 1)
 
-            mask_w(1, 0, 0)
-            mask_w(1, 0, 1)
+            mask_w(1, 0)
             transpose_grad(1)
             group_grad(1)
-            quantise_w(1, 0, 1)
-            quantise_w(1, 0, 0)
-            mask_w(1, 1, 0)
+            quantise_w(1, 0)
             quantise_grad(1)
+            mask_w(1, 1)
 
             multiply(0, 0, (0, 1))
             multiply(1, 0, (0, 1))
             transpose_grad(2)
             transpose_grad(3)
-            empty(0, 0, "VS")
-            quantise_w(1, 1, 0)
-            mask_w(1, 1, 1)
-            empty(1, 0, "VS")
+            empty(0, 0, "SV", (0,))
+            empty(1, 0, "SV", (0,))
             group_grad(2)
+            empty(0, 0, "SV", (1,))
+            quantise_w(1, 1)
             quantise_grad(2)
+            empty(1, 0, "SV", (1,))
             group_grad(3)
-            quantise_w(1, 1, 1)
             quantise_grad(3)
             multiply(2, 0, (0, 1))
             multiply(3, 0, (0, 1))
             empty(2, 0, "SS")
 
-            mask_w(2, 1, 0)
+            mask_w(2, 1)
             empty(3, 0, "SS")
-            mask_w(2, 1, 1)
             multiply(0, 1, (0, 1))
             multiply(1, 1, (0, 1))
-            quantise_w(2, 1, 0)
-            quantise_w(2, 1, 1)
-            mask_w(1, 2, 0)
-            mask_w(1, 2, 1)
+            quantise_w(2, 1)
+            mask_w(1, 2)
             multiply(0, 1, (2,))
             multiply(1, 1, (2,))
-            quantise_w(1, 2, 0)
-            quantise_w(1, 2, 1)
+            quantise_w(1, 2)
             empty(0, 1, "SS")
             empty(1, 1, "SS")
-            mask_w(2, 2, 0)
-            mask_w(2, 2, 1)
+            mask_w(2, 2)
             store(2, 0)
             store(3, 0)
             store(0, 0)
@@ -264,8 +260,7 @@ def tile_skeletonlinear_t_kernel(tc, x, weight, mask, bias, grad_out, out):
             multiply(2, 1, (0, 1, 2))
             multiply(3, 1, (0, 1, 2))
             transpose_grad(4)
-            quantise_w(2, 2, 0)
-            quantise_w(2, 2, 1)
+            quantise_w(2, 2)
             empty(2, 1, "SS")
             group_grad(4)
             quantise_grad(4)
@@ -296,5 +291,4 @@ def tile_skeletonlinear_t_kernel(tc, x, weight, mask, bias, grad_out, out):
                         group_grad(i + 2)
                     if k == 2 and i + 2 < PAIRS:
                         quantise_grad(i + 2)
-                    if k + 1 == sum(stores_of(i)[k]):
-                        store(i, stores_of(i)[k][0])
+                    store_if_last(i, k)

@@ -39,10 +39,10 @@ def tile_skeletonlinear_t_kernel(tc, x, weight, mask, bias, grad_out, out):
         grad_stage = pools.enter_context(tc.tile_pool(name="grad_stage", bufs=3))
         w_stage = pools.enter_context(tc.tile_pool(name="w_stage", bufs=4))
         results = pools.enter_context(tc.tile_pool(name="results", bufs=4))
-        wide_results = pools.enter_context(tc.tile_pool(name="wide_results", bufs=4))
+        wide_results = pools.enter_context(tc.tile_pool(name="wide_results", bufs=3))
+        row_results = pools.enter_context(tc.tile_pool(name="row_results", bufs=2))
         mask_stage = pools.enter_context(tc.tile_pool(name="mask_stage", bufs=2))
-        flipped = pools.enter_context(tc.psum_pool(name="flipped", bufs=3))
-        sums = pools.enter_context(tc.psum_pool(name="sums", bufs=5))
+        psum = pools.enter_context(tc.psum_pool(name="psum", bufs=8))
 
         identity = keep.tile([P, P], F32)
         make_identity(nc, identity[:])
@@ -70,8 +70,8 @@ def tile_skeletonlinear_t_kernel(tc, x, weight, mask, bias, grad_out, out):
 
         def load_w(r, cols):
             first, width = cols[0] * CH, len(cols) * CH
-            weight_rows = keep.tile([P, PACK, width], BF16, name="weight_raw_%d_%d" % (r, cols[0]))
-            mask_rows = keep.tile([P, PACK, width], BF16, name="mask_raw_%d_%d" % (r, cols[0]))
+            weight_rows = keep.tile([P, PACK, width], BF16, name="weight_raw_%d" % width)
+            mask_rows = keep.tile([P, PACK, width], BF16, name="mask_raw_%d" % width)
             for u in range(2):
                 top = r * CH + u * HALF
                 for raw, source in ((weight_rows, weight), (mask_rows, mask)):
@@ -93,7 +93,7 @@ def tile_skeletonlinear_t_kernel(tc, x, weight, mask, bias, grad_out, out):
             grouped = w_stage.tile([P, CH, PACK], BF16, align_bytes=64)
             grouped_w[(r, k)] = grouped
             start = 0
-            if (r, k) in ((1, 0),):
+            if (r, k) in ((1, 0), (2, 1)):
                 start = HALF
                 masked = mask_stage.tile([P, PACK, HALF], BF16)
                 nc.vector.tensor_tensor(
@@ -119,7 +119,7 @@ def tile_skeletonlinear_t_kernel(tc, x, weight, mask, bias, grad_out, out):
 
         def transpose_grad(i):
             for g in range(JOINTS):
-                bank = flipped.tile([P, 4 * P], F32)
+                bank = psum.tile([P, 4 * P], F32, name="bank")
                 for a in range(2):
                     for u in range(2):
                         nc.tensor.transpose(
@@ -151,7 +151,7 @@ def tile_skeletonlinear_t_kernel(tc, x, weight, mask, bias, grad_out, out):
         def multiply(i, k, rows):
             for a in range(2):
                 if rows[0] == neighbours(k)[0]:
-                    acc = sums.tile([P, CH], F32)
+                    acc = psum.tile([P, CH], F32, name="bank")
                     accs[(i, k, a)] = acc
                 for r in rows:
                     columns = slice((2 * r + a) * P, (2 * r + a + 1) * P)
@@ -168,7 +168,7 @@ def tile_skeletonlinear_t_kernel(tc, x, weight, mask, bias, grad_out, out):
         def empty(i, k, engines, parts=(0, 1)):
             first, width = stores_of(i)[k]
             if (i, first) not in tiles:
-                pool = results if width == 1 else wide_results
+                pool = (results, wide_results, row_results)[width - 1]
                 tiles[(i, first)] = pool.tile([P, 2, width * CH], F32, name="result_%d" % width)
             result = tiles[(i, first)]
             at = (k - first) * CH
@@ -188,8 +188,8 @@ def tile_skeletonlinear_t_kernel(tc, x, weight, mask, bias, grad_out, out):
                     nc.sync.dma_start(out=out_tiles[:, 2 * i + a, columns], in_=tiles[(i, first)][:, a, :])
 
         def stores_of(i):
-            if i in (2, 3):
-                return ((0, 1), (1, 2), (1, 2))
+            if i in (3, 4):
+                return ((0, 3), (0, 3), (0, 3))
             if i == 6:
                 return ((0, 1), (1, 1), (2, 1))
             return ((0, 2), (0, 2), (2, 1))
@@ -235,16 +235,17 @@ def tile_skeletonlinear_t_kernel(tc, x, weight, mask, bias, grad_out, out):
             quantise_w(1, 1)
             quantise_grad(2)
             empty(1, 0, "SV", (1,))
+            multiply(0, 1, (0, 1))
             group_grad(3)
             quantise_grad(3)
             multiply(2, 0, (0, 1))
-            multiply(3, 0, (0, 1))
             empty(2, 0, "SS")
+            multiply(1, 1, (0, 1))
 
             mask_w(2, 1)
+            multiply(3, 0, (0, 1))
             empty(3, 0, "SS")
-            multiply(0, 1, (0, 1))
-            multiply(1, 1, (0, 1))
+            multiply(2, 1, (0, 1))
             quantise_w(2, 1)
             mask_w(1, 2)
             multiply(0, 1, (2,))
@@ -253,33 +254,32 @@ def tile_skeletonlinear_t_kernel(tc, x, weight, mask, bias, grad_out, out):
             empty(0, 1, "SS")
             empty(1, 1, "SS")
             mask_w(2, 2)
-            store(2, 0)
-            store(3, 0)
-            store(0, 0)
-            store(1, 0)
-            multiply(2, 1, (0, 1, 2))
+            store_if_last(0, 1)
+            store_if_last(1, 1)
+            multiply(2, 1, (2,))
             multiply(3, 1, (0, 1, 2))
             transpose_grad(4)
+            transpose_grad(5)
             quantise_w(2, 2)
             empty(2, 1, "SS")
             group_grad(4)
             quantise_grad(4)
             empty(3, 1, "SS")
+            store_if_last(2, 1)
             multiply(0, 2, (1, 2))
             multiply(1, 2, (1, 2))
-            transpose_grad(5)
             empty(0, 2, "VS")
-            store(0, 2)
+            store_if_last(0, 2)
             empty(1, 2, "VS")
-            store(1, 2)
+            store_if_last(1, 2)
             multiply(2, 2, (1, 2))
             multiply(3, 2, (1, 2))
             group_grad(5)
             empty(2, 2, "VS")
-            store(2, 1)
+            store_if_last(2, 2)
             quantise_grad(5)
             empty(3, 2, "VS")
-            store(3, 1)
+            store_if_last(3, 2)
 
             for i in range(4, PAIRS):
                 for k in range(JOINTS):

@@ -29,19 +29,25 @@ def neighbours(joint):
     return [j for j in (joint - 1, joint, joint + 1) if 0 <= j < JOINTS]
 
 
+def pieces_of(i):
+    if i == 4:
+        return ((0, 6),)
+    if i in (0, 6, 7):
+        return ((0, 2), (2, 3), (3, 5), (5, 6))
+    return ((0, 2), (2, 6))
+
+
 def tile_skeletonlinear_t_kernel(tc, x, weight, mask, bias, grad_out, out):
     nc = tc.nc
-    grad_tiles = grad_out.rearrange("(p t) c -> p t c", t=TILES)
-    out_tiles = out.rearrange("(p t) c -> p t c", t=TILES)
+    grad_rows = grad_out.rearrange("(p t) c -> p (t c)", t=TILES)
+    out_rows = out.rearrange("(p t) c -> p (t c)", t=TILES)
 
     with ExitStack() as pools:
         keep = pools.enter_context(tc.tile_pool(name="keep", bufs=1))
         grad_stage = pools.enter_context(tc.tile_pool(name="grad_stage", bufs=3))
         w_stage = pools.enter_context(tc.tile_pool(name="w_stage", bufs=4))
-        results = pools.enter_context(tc.tile_pool(name="results", bufs=4))
-        wide_results = pools.enter_context(tc.tile_pool(name="wide_results", bufs=3))
-        row_results = pools.enter_context(tc.tile_pool(name="row_results", bufs=2))
         mask_stage = pools.enter_context(tc.tile_pool(name="mask_stage", bufs=2))
+        results = pools.enter_context(tc.tile_pool(name="results", bufs=5))
         psum = pools.enter_context(tc.psum_pool(name="psum", bufs=8))
 
         identity = keep.tile([P, P], F32)
@@ -58,17 +64,22 @@ def tile_skeletonlinear_t_kernel(tc, x, weight, mask, bias, grad_out, out):
 
         grad_words = {}
         w_raw = {}
+        grouped_w = {}
+        turned_grad = {}
+        grouped_grad = {}
+        sums = {}
+        result_rows = {}
+        emptied = set()
 
         def load_grad(first, count):
             raw = keep.tile([P, count * WIDTH], BF16, name="grad_raw_%d" % first)
-            nc.sync.dma_start(
-                out=raw[:].rearrange("p (a c) -> p a c", a=count), in_=grad_tiles[:, first : first + count, :]
-            )
+            nc.sync.dma_start(out=raw[:], in_=grad_rows[:, first * WIDTH : (first + count) * WIDTH])
             words = raw[:].bitcast(F32)
             for a in range(count):
                 grad_words[first + a] = words[:, a * (WIDTH // 2) : (a + 1) * (WIDTH // 2)]
 
-        def load_w(r, cols):
+        def load_w(r):
+            cols = neighbours(r)
             first, width = cols[0] * CH, len(cols) * CH
             weight_rows = keep.tile([P, PACK, width], BF16, name="weight_raw_%d" % width)
             mask_rows = keep.tile([P, PACK, width], BF16, name="mask_raw_%d" % width)
@@ -81,12 +92,6 @@ def tile_skeletonlinear_t_kernel(tc, x, weight, mask, bias, grad_out, out):
                     )
             for n, k in enumerate(cols):
                 w_raw[(r, k)] = (weight_rows, mask_rows, n * CH)
-
-        grouped_w = {}
-        banks = {}
-        grouped_grad = {}
-        accs = {}
-        tiles = {}
 
         def mask_w(r, k):
             weight_rows, mask_rows, base = w_raw[(r, k)]
@@ -120,6 +125,7 @@ def tile_skeletonlinear_t_kernel(tc, x, weight, mask, bias, grad_out, out):
         def transpose_grad(i):
             for g in range(JOINTS):
                 bank = psum.tile([P, 4 * P], F32, name="bank")
+                turned_grad[(i, g)] = bank
                 for a in range(2):
                     for u in range(2):
                         nc.tensor.transpose(
@@ -127,7 +133,6 @@ def tile_skeletonlinear_t_kernel(tc, x, weight, mask, bias, grad_out, out):
                             in_=grad_words[2 * i + a][:, g * HALF + u * P : g * HALF + (u + 1) * P],
                             identity=identity[:],
                         )
-                banks[(i, g)] = bank
 
         def group_grad(i):
             grouped = grad_stage.tile([P, JOINTS * 2 * P * PACK], BF16, align_bytes=64, name="grad_grouped")
@@ -136,7 +141,7 @@ def tile_skeletonlinear_t_kernel(tc, x, weight, mask, bias, grad_out, out):
             for g in range(JOINTS):
                 nc.scalar.copy(
                     out=words[:, g * 4 * P : (g + 1) * 4 * P].rearrange("p (a r u) -> p a r u", a=2, u=2),
-                    in_=banks[(i, g)][:].rearrange("p (a u r) -> p a r u", a=2, u=2),
+                    in_=turned_grad[(i, g)][:].rearrange("p (a u r) -> p a r u", a=2, u=2),
                 )
 
         def quantise_grad(i):
@@ -148,15 +153,15 @@ def tile_skeletonlinear_t_kernel(tc, x, weight, mask, bias, grad_out, out):
                     in_=grouped_grad[i][:, first * 2 * P * PACK : (first + count) * 2 * P * PACK],
                 )
 
-        def multiply(i, k, rows):
-            for a in range(2):
+        def multiply(i, k, rows, parts=(0, 1)):
+            for a in parts:
                 if rows[0] == neighbours(k)[0]:
                     acc = psum.tile([P, CH], F32, name="bank")
-                    accs[(i, k, a)] = acc
+                    sums[(i, a, k)] = acc
                 for r in rows:
                     columns = slice((2 * r + a) * P, (2 * r + a + 1) * P)
                     nc.tensor.matmul_mx(
-                        out=accs[(i, k, a)][:],
+                        out=sums[(i, a, k)][:],
                         lhsT=grad_codes[:, i, columns].bitcast(E5M2X4),
                         lhsT_scale=grad_scales[:, i, columns],
                         rhs=w_codes[(r, k)][:].bitcast(E4M3X4),
@@ -166,46 +171,33 @@ def tile_skeletonlinear_t_kernel(tc, x, weight, mask, bias, grad_out, out):
                     )
 
         def empty(i, k, engines, parts=(0, 1)):
-            first, width = stores_of(i)[k]
-            if (i, first) not in tiles:
-                pool = (results, wide_results, row_results)[width - 1]
-                tiles[(i, first)] = pool.tile([P, 2, width * CH], F32, name="result_%d" % width)
-            result = tiles[(i, first)]
-            at = (k - first) * CH
-            for a in parts:
-                if engines[a] == "S":
-                    nc.scalar.copy(out=result[:, a, at : at + CH], in_=accs[(i, k, a)][:])
+            if i not in result_rows:
+                result_rows[i] = results.tile([P, 2 * WIDTH], F32, name="result")
+            for a, engine in zip(parts, engines):
+                block = result_rows[i][:, (JOINTS * a + k) * CH : (JOINTS * a + k + 1) * CH]
+                if engine == "S":
+                    nc.scalar.copy(out=block, in_=sums[(i, a, k)][:])
                 else:
-                    nc.vector.tensor_copy(out=result[:, a, at : at + CH], in_=accs[(i, k, a)][:])
+                    nc.vector.tensor_copy(out=block, in_=sums[(i, a, k)][:])
 
-        def store(i, first):
-            width = stores_of(i)[first][1]
-            columns = slice(first * CH, (first + width) * CH)
-            if i < PAIRS - 1:
-                nc.sync.dma_start(out=out_tiles[:, 2 * i : 2 * i + 2, columns], in_=tiles[(i, first)][:])
-            else:
-                for a in range(2):
-                    nc.sync.dma_start(out=out_tiles[:, 2 * i + a, columns], in_=tiles[(i, first)][:, a, :])
-
-        def stores_of(i):
-            if i in (3, 4):
-                return ((0, 3), (0, 3), (0, 3))
-            if i == 6:
-                return ((0, 1), (1, 1), (2, 1))
-            return ((0, 2), (0, 2), (2, 1))
-
-        def store_if_last(i, k):
-            first, width = stores_of(i)[k]
-            if k == first + width - 1:
-                store(i, first)
+        def store(i, k, parts=(0, 1)):
+            for a in parts:
+                emptied.add((i, JOINTS * a + k))
+                for first, end in pieces_of(i):
+                    if first <= JOINTS * a + k < end and all((i, b) in emptied for b in range(first, end)):
+                        at = 2 * i * WIDTH
+                        nc.sync.dma_start(
+                            out=out_rows[:, at + first * CH : at + end * CH],
+                            in_=result_rows[i][:, first * CH : end * CH],
+                        )
 
         with tc.manual_schedule():
-            load_w(0, [0, 1])
+            load_w(0)
             load_grad(0, 2)
-            load_w(1, [0, 1, 2])
+            load_w(1)
             load_grad(2, 2)
             load_grad(4, 4)
-            load_w(2, [1, 2])
+            load_w(2)
             load_grad(8, 4)
             load_grad(12, 4)
 
@@ -228,13 +220,13 @@ def tile_skeletonlinear_t_kernel(tc, x, weight, mask, bias, grad_out, out):
             multiply(1, 0, (0, 1))
             transpose_grad(2)
             transpose_grad(3)
-            empty(0, 0, "SV", (0,))
-            empty(1, 0, "SV", (0,))
+            empty(0, 0, "S", (0,))
+            empty(1, 0, "S", (0,))
             group_grad(2)
-            empty(0, 0, "SV", (1,))
+            empty(0, 0, "V", (1,))
             quantise_w(1, 1)
             quantise_grad(2)
-            empty(1, 0, "SV", (1,))
+            empty(1, 0, "V", (1,))
             multiply(0, 1, (0, 1))
             group_grad(3)
             quantise_grad(3)
@@ -254,8 +246,10 @@ def tile_skeletonlinear_t_kernel(tc, x, weight, mask, bias, grad_out, out):
             empty(0, 1, "SS")
             empty(1, 1, "SS")
             mask_w(2, 2)
-            store_if_last(0, 1)
-            store_if_last(1, 1)
+            for i in range(4):
+                store(i, 0)
+            store(0, 1)
+            store(1, 1)
             multiply(2, 1, (2,))
             multiply(3, 1, (0, 1, 2))
             transpose_grad(4)
@@ -265,30 +259,33 @@ def tile_skeletonlinear_t_kernel(tc, x, weight, mask, bias, grad_out, out):
             group_grad(4)
             quantise_grad(4)
             empty(3, 1, "SS")
-            store_if_last(2, 1)
+            store(2, 1)
+            store(3, 1)
             multiply(0, 2, (1, 2))
             multiply(1, 2, (1, 2))
-            empty(0, 2, "VS")
-            store_if_last(0, 2)
-            empty(1, 2, "VS")
-            store_if_last(1, 2)
+            empty(0, 2, "SV")
+            store(0, 2)
+            empty(1, 2, "SV")
+            store(1, 2)
             multiply(2, 2, (1, 2))
             multiply(3, 2, (1, 2))
             group_grad(5)
-            empty(2, 2, "VS")
-            store_if_last(2, 2)
+            empty(2, 2, "SV")
+            store(2, 2)
             quantise_grad(5)
-            empty(3, 2, "VS")
-            store_if_last(3, 2)
+            empty(3, 2, "SV")
+            store(3, 2)
 
             for i in range(4, PAIRS):
-                for k in range(JOINTS):
-                    multiply(i, k, neighbours(k))
-                    if k == 1 and i + 2 < PAIRS:
-                        transpose_grad(i + 2)
-                    empty(i, k, ("VS", "SS", "VS")[k])
-                    if k == 1 and i + 2 < PAIRS:
-                        group_grad(i + 2)
-                    if k == 2 and i + 2 < PAIRS:
-                        quantise_grad(i + 2)
-                    store_if_last(i, k)
+                for a in range(2):
+                    for k in range(JOINTS):
+                        last = (a, k) == (1, JOINTS - 1)
+                        multiply(i, k, neighbours(k), (a,))
+                        if last and i + 2 < PAIRS:
+                            transpose_grad(i + 2)
+                        empty(i, k, ("V", "S")[(a + k) % 2], (a,))
+                        if last and i + 2 < PAIRS:
+                            group_grad(i + 2)
+                        if (a, k) == (0, 0) and 6 <= i + 1 < PAIRS:
+                            quantise_grad(i + 1)
+                        store(i, k, (a,))

from contextlib import ExitStack

import concourse.mybir as mybir
from concourse.masks import make_identity

F32 = mybir.dt.float32
BF16 = mybir.dt.bfloat16
U32 = mybir.dt.uint32
U8 = mybir.dt.uint8
E4M3X4 = mybir.dt.float8_e4m3fn_x4
E5M2X4 = mybir.dt.float8_e5m2_x4

P = 128
PACK = 4
JOINTS = 3
CH = 512
WIDTH = JOINTS * CH
TOKENS = 2048
TILES = TOKENS // P
PAIRS = TILES // 2
HALF = CH // 2
BLOCKS = 7

FLOPS = 2 * TOKENS * CH * CH * BLOCKS
BYTES = 2 * TOKENS * WIDTH + 2 * 2 * BLOCKS * CH * CH + 4 * TOKENS * WIDTH


def neighbours(joint):
    return [j for j in (joint - 1, joint, joint + 1) if 0 <= j < JOINTS]


def pieces_of(i):
    if i == 4:
        return ((0, 6),)
    if i in (0, 6, 7):
        return ((0, 2), (2, 3), (3, 5), (5, 6))
    return ((0, 2), (2, 6))


def tile_skeletonlinear_t_kernel(tc, x, weight, mask, bias, grad_out, out):
    nc = tc.nc
    grad_rows = grad_out.rearrange("(p t) c -> p (t c)", t=TILES)
    out_rows = out.rearrange("(p t) c -> p (t c)", t=TILES)

    with ExitStack() as pools:
        keep = pools.enter_context(tc.tile_pool(name="keep", bufs=1))
        grad_stage = pools.enter_context(tc.tile_pool(name="grad_stage", bufs=3))
        w_stage = pools.enter_context(tc.tile_pool(name="w_stage", bufs=4))
        mask_stage = pools.enter_context(tc.tile_pool(name="mask_stage", bufs=2))
        results = pools.enter_context(tc.tile_pool(name="results", bufs=5))
        psum = pools.enter_context(tc.psum_pool(name="psum", bufs=8))

        identity = keep.tile([P, P], F32)
        make_identity(nc, identity[:])

        grad_codes = keep.tile([P, PAIRS, JOINTS * 2 * P], U32, align_bytes=64)
        grad_scales = keep.tile([P, PAIRS, JOINTS * 2 * P], U8, align_bytes=64)
        w_codes = {}
        w_scales = {}
        for r in range(JOINTS):
            for k in neighbours(r):
                w_codes[(r, k)] = keep.tile([P, CH], U32, align_bytes=64, name="w_codes_%d_%d" % (r, k))
                w_scales[(r, k)] = keep.tile([P, CH], U8, align_bytes=64, name="w_scales_%d_%d" % (r, k))

        grad_words = {}
        w_raw = {}
        grouped_w = {}
        turned_grad = {}
        grouped_grad = {}
        sums = {}
        result_rows = {}
        emptied = set()

        def load_grad(first, count):
            raw = keep.tile([P, count * WIDTH], BF16, name="grad_raw_%d" % first)
            nc.sync.dma_start(out=raw[:], in_=grad_rows[:, first * WIDTH : (first + count) * WIDTH])
            words = raw[:].bitcast(F32)
            for a in range(count):
                grad_words[first + a] = words[:, a * (WIDTH // 2) : (a + 1) * (WIDTH // 2)]

        def load_w(r):
            cols = neighbours(r)
            first, width = cols[0] * CH, len(cols) * CH
            weight_rows = keep.tile([P, PACK, width], BF16, name="weight_raw_%d" % width)
            mask_rows = keep.tile([P, PACK, width], BF16, name="mask_raw_%d" % width)
            for u in range(2):
                top = r * CH + u * HALF
                for raw, source in ((weight_rows, weight), (mask_rows, mask)):
                    nc.sync.dma_start(
                        out=raw[:, 2 * u : 2 * u + 2, :],
                        in_=source[top : top + HALF, first : first + width].rearrange("(p e) c -> p e c", e=2),
                    )
            for n, k in enumerate(cols):
                w_raw[(r, k)] = (weight_rows, mask_rows, n * CH)

        def mask_w(r, k):
            weight_rows, mask_rows, base = w_raw[(r, k)]
            grouped = w_stage.tile([P, CH, PACK], BF16, align_bytes=64)
            grouped_w[(r, k)] = grouped
            start = 0
            if (r, k) in ((1, 0), (2, 1)):
                start = HALF
                masked = mask_stage.tile([P, PACK, HALF], BF16)
                nc.vector.tensor_tensor(
                    out=masked[:],
                    in0=weight_rows[:, :, base : base + HALF],
                    in1=mask_rows[:, :, base : base + HALF],
                    op=mybir.AluOpType.mult,
                )
                nc.scalar.copy(out=grouped[:, 0:HALF, :], in_=masked[:].rearrange("p t c -> p c t"))
            nc.vector.tensor_tensor(
                out=grouped[:, start:CH, :],
                in0=weight_rows[:, :, base + start : base + CH].rearrange("p t c -> p c t"),
                in1=mask_rows[:, :, base + start : base + CH].rearrange("p t c -> p c t"),
                op=mybir.AluOpType.mult,
            )

        def quantise_w(r, k):
            nc.vector.quantize_mx(
                out=w_codes[(r, k)][:].bitcast(E4M3X4),
                scales=w_scales[(r, k)][:],
                in_=grouped_w[(r, k)][:].rearrange("p c t -> p (c t)"),
            )

        def transpose_grad(i):
            for g in range(JOINTS):
                bank = psum.tile([P, 4 * P], F32, name="bank")
                turned_grad[(i, g)] = bank
                for a in range(2):
                    for u in range(2):
                        nc.tensor.transpose(
                            out=bank[:, (2 * a + u) * P : (2 * a + u + 1) * P],
                            in_=grad_words[2 * i + a][:, g * HALF + u * P : g * HALF + (u + 1) * P],
                            identity=identity[:],
                        )

        def group_grad(i):
            grouped = grad_stage.tile([P, JOINTS * 2 * P * PACK], BF16, align_bytes=64, name="grad_grouped")
            grouped_grad[i] = grouped
            words = grouped[:].bitcast(F32)
            for g in range(JOINTS):
                nc.scalar.copy(
                    out=words[:, g * 4 * P : (g + 1) * 4 * P].rearrange("p (a r u) -> p a r u", a=2, u=2),
                    in_=turned_grad[(i, g)][:].rearrange("p (a u r) -> p a r u", a=2, u=2),
                )

        def quantise_grad(i):
            for first, count in ((0, 2), (2, 1)):
                columns = slice(first * 2 * P, (first + count) * 2 * P)
                nc.vector.quantize_mx(
                    out=grad_codes[:, i, columns].bitcast(E5M2X4),
                    scales=grad_scales[:, i, columns],
                    in_=grouped_grad[i][:, first * 2 * P * PACK : (first + count) * 2 * P * PACK],
                )

        def multiply(i, k, rows, parts=(0, 1)):
            for a in parts:
                if rows[0] == neighbours(k)[0]:
                    acc = psum.tile([P, CH], F32, name="bank")
                    sums[(i, a, k)] = acc
                for r in rows:
                    columns = slice((2 * r + a) * P, (2 * r + a + 1) * P)
                    nc.tensor.matmul_mx(
                        out=sums[(i, a, k)][:],
                        lhsT=grad_codes[:, i, columns].bitcast(E5M2X4),
                        lhsT_scale=grad_scales[:, i, columns],
                        rhs=w_codes[(r, k)][:].bitcast(E4M3X4),
                        rhs_scale=w_scales[(r, k)][:],
                        start=(r == neighbours(k)[0]),
                        stop=(r == neighbours(k)[-1]),
                    )

        def empty(i, k, engines, parts=(0, 1)):
            if i not in result_rows:
                result_rows[i] = results.tile([P, 2 * WIDTH], F32, name="result")
            for a, engine in zip(parts, engines):
                block = result_rows[i][:, (JOINTS * a + k) * CH : (JOINTS * a + k + 1) * CH]
                if engine == "S":
                    nc.scalar.copy(out=block, in_=sums[(i, a, k)][:])
                else:
                    nc.vector.tensor_copy(out=block, in_=sums[(i, a, k)][:])

        def store(i, k, parts=(0, 1)):
            for a in parts:
                emptied.add((i, JOINTS * a + k))
                for first, end in pieces_of(i):
                    if first <= JOINTS * a + k < end and all((i, b) in emptied for b in range(first, end)):
                        at = 2 * i * WIDTH
                        nc.sync.dma_start(
                            out=out_rows[:, at + first * CH : at + end * CH],
                            in_=result_rows[i][:, first * CH : end * CH],
                        )

        with tc.manual_schedule():
            load_w(0)
            load_grad(0, 2)
            load_w(1)
            load_grad(2, 2)
            load_grad(4, 4)
            load_w(2)
            load_grad(8, 4)
            load_grad(12, 4)

            transpose_grad(0)
            group_grad(0)
            mask_w(0, 0)
            quantise_w(0, 0)
            quantise_grad(0)
            mask_w(0, 1)
            quantise_w(0, 1)

            mask_w(1, 0)
            transpose_grad(1)
            group_grad(1)
            quantise_w(1, 0)
            quantise_grad(1)
            mask_w(1, 1)

            multiply(0, 0, (0, 1))
            multiply(1, 0, (0, 1))
            transpose_grad(2)
            transpose_grad(3)
            empty(0, 0, "S", (0,))
            empty(1, 0, "S", (0,))
            group_grad(2)
            empty(0, 0, "V", (1,))
            quantise_w(1, 1)
            quantise_grad(2)
            empty(1, 0, "V", (1,))
            multiply(0, 1, (0, 1))
            group_grad(3)
            quantise_grad(3)
            multiply(2, 0, (0, 1))
            empty(2, 0, "SS")
            multiply(1, 1, (0, 1))

            mask_w(2, 1)
            multiply(3, 0, (0, 1))
            empty(3, 0, "SS")
            multiply(2, 1, (0, 1))
            quantise_w(2, 1)
            mask_w(1, 2)
            multiply(0, 1, (2,))
            multiply(1, 1, (2,))
            quantise_w(1, 2)
            empty(0, 1, "SS")
            empty(1, 1, "SS")
            mask_w(2, 2)
            for i in range(4):
                store(i, 0)
            store(0, 1)
            store(1, 1)
            multiply(2, 1, (2,))
            multiply(3, 1, (0, 1, 2))
            transpose_grad(4)
            transpose_grad(5)
            quantise_w(2, 2)
            empty(2, 1, "SS")
            group_grad(4)
            quantise_grad(4)
            empty(3, 1, "SS")
            store(2, 1)
            store(3, 1)
            multiply(0, 2, (1, 2))
            multiply(1, 2, (1, 2))
            empty(0, 2, "SV")
            store(0, 2)
            empty(1, 2, "SV")
            store(1, 2)
            multiply(2, 2, (1, 2))
            multiply(3, 2, (1, 2))
            group_grad(5)
            empty(2, 2, "SV")
            store(2, 2)
            quantise_grad(5)
            empty(3, 2, "SV")
            store(3, 2)

            for i in range(4, PAIRS):
                for a in range(2):
                    for k in range(JOINTS):
                        last = (a, k) == (1, JOINTS - 1)
                        multiply(i, k, neighbours(k), (a,))
                        if last and i + 2 < PAIRS:
                            transpose_grad(i + 2)
                        empty(i, k, ("V", "S")[(a + k) % 2], (a,))
                        if last and i + 2 < PAIRS:
                            group_grad(i + 2)
                        if (a, k) == (0, 0) and 6 <= i + 1 < PAIRS:
                            quantise_grad(i + 1)
                        store(i, k, (a,))
